import numpy as np
import ml_dtypes


def mxq(x, axis, fmt="e4m3"):
    dtype, down = {"e4m3": (ml_dtypes.float8_e4m3fn, 7), "e5m2": (ml_dtypes.float8_e5m2, 14)}[fmt]
    v = np.moveaxis(np.asarray(x, np.float32).astype(ml_dtypes.bfloat16).astype(np.float64), axis, -1)
    blocks = v.reshape(v.shape[:-1] + (-1, 32))
    amax = np.abs(blocks).max(-1, keepdims=True)
    byte = np.maximum(np.where(amax > 0, np.frexp(amax)[1] - 1 + 127, 0) - down, 1)
    scale = np.exp2(byte - 127.0)
    codes = (blocks / scale).astype(np.float32).astype(dtype).astype(np.float64)
    return np.moveaxis((codes * scale).reshape(v.shape), -1, axis)


WIDE = False


def mx_kscale(k):
    if not WIDE:
        return np.ones(k)
    levels = np.array([10, -10, 5, -5, 0])
    a = np.random.permutation(np.resize(levels, k // 512 * 4)).reshape(k // 512, 4)
    idx = np.arange(k)
    return np.exp2(a[idx // 512, idx % 128 // 32])


BF16 = ml_dtypes.bfloat16


def bf(x):
    return np.asarray(x, np.float32).astype(BF16)


def f64(x):
    return np.asarray(x).astype(np.float64)


E2M1 = np.array([0.0, 0.5, 1.0, 1.5, 2.0, 3.0, 4.0, 6.0, -0.0, -0.5, -1.0, -1.5, -2.0, -3.0, -4.0, -6.0])


def pack_weight(w, fmt):
    k, n = w.shape
    w = f64(bf(w)).reshape(k // 32, 32, n)
    amax = np.abs(w).max(1)
    if fmt == "e4m3":
        byte = np.frexp(amax)[1] - 1 + 127 - 7
    else:
        mant, ex = np.frexp(amax / 6.0)
        byte = np.where(mant > 0.5, ex, ex - 1) + 127
    byte = np.clip(np.where(amax > 0, byte, 1), 1, 254)
    scaled = (w * np.exp2(127.0 - byte)[:, None, :]).reshape(k, n).astype(np.float32)
    by_word = np.ascontiguousarray(scaled.reshape(k // 512, 128, 4, n).transpose(0, 1, 3, 2))
    if fmt == "e4m3":
        words = by_word.astype(ml_dtypes.float8_e4m3fn).view(np.uint8)
    else:
        c = by_word.astype(ml_dtypes.float4_e2m1fn).view(np.uint8) & 0xF
        words = c[..., 0::2] | (c[..., 1::2] << 4)
    return np.ascontiguousarray(words), np.ascontiguousarray(byte.astype(np.uint8).reshape(k // 512, 16, n))


def unpack_weight(words, scales, fmt):
    g, p, n, _ = words.shape
    if fmt == "e4m3":
        vals = np.ascontiguousarray(words).view(ml_dtypes.float8_e4m3fn).astype(np.float64)
    else:
        nib = np.empty((g, p, n, 4), np.uint8)
        nib[..., 0::2] = words & 0xF
        nib[..., 1::2] = words >> 4
        vals = E2M1[nib]
    vals = vals * np.repeat(np.exp2(scales.astype(np.float64) - 127.0), 8, axis=1)[..., None]
    return vals.transpose(0, 1, 3, 2).reshape(g * 512, n)

def pack4(w):
    words, scales = pack_weight(w, "e2m1")
    return words.reshape(words.shape[0], 128, -1), scales


def unpack4(words, scales):
    return unpack_weight(words.reshape(words.shape[0], 128, -1, 2), scales, "e2m1")


B, T, HS, WS, C, HN, D = 1, 8, 4, 4, 16384, 24, 64
N = T * HS * WS
E = HN * D
EPS = 1e-6
BASE = 10000.0


def axis_angles(n, dim):
    f = 1.0 / BASE ** (np.arange(0, dim, 2)[: dim // 2] / dim)
    return np.repeat(np.arange(n)[:, None] * f[None, :], 2, axis=-1)


def rope_angles():
    dim_t = D - 4 * (D // 6)
    dim_h = 2 * (D // 6)
    dim_w = 2 * (D // 6)
    at = np.broadcast_to(axis_angles(T, dim_t)[:, None, None, :], (T, HS, WS, dim_t))
    ah = np.broadcast_to(axis_angles(HS, dim_h)[None, :, None, :], (T, HS, WS, dim_h))
    aw = np.broadcast_to(axis_angles(WS, dim_w)[None, None, :, :], (T, HS, WS, dim_w))
    return np.concatenate([at, ah, aw], axis=-1).reshape(N, D)


def rotate_half(v):
    p = v.reshape(v.shape[:-1] + (v.shape[-1] // 2, 2))
    return np.stack((-p[..., 1], p[..., 0]), axis=-1).reshape(v.shape)


def setup_inputs():
    s = mx_kscale(C)
    x = bf(np.random.standard_normal((B, N, C)) * s)
    w = np.random.standard_normal((E, C)) / np.sqrt(C) / s[None, :]
    w_words, w_scales = pack4(np.ascontiguousarray(w.T))
    b = bf(np.random.standard_normal(E) * 0.3)
    norm_w = bf(1.0 + 0.1 * np.random.standard_normal(D))
    return {"x": x,
            "w_words": w_words,
            "w_scales": w_scales,
            "b": b,
            "norm_w": norm_w}


def reference(x, w_words, w_scales, b, norm_w):
    y = (mxq(f64(x), 2, "e4m3") @ unpack4(w_words, w_scales)) + f64(b)
    y = y.reshape(B, N, HN, D).transpose(0, 2, 1, 3)
    u = y / np.sqrt(np.mean(y * y, axis=-1, keepdims=True) + EPS) * f64(norm_w)
    a = rope_angles()
    return u * np.cos(a) + rotate_half(u) * np.sin(a)

@@ -1,0 +1,300 @@
+import math
+from contextlib import ExitStack
+
+import concourse.mybir as mybir
+from concourse.masks import make_identity
+
+F32 = mybir.dt.float32
+BF16 = mybir.dt.bfloat16
+I32 = mybir.dt.int32
+U32 = mybir.dt.uint32
+U8 = mybir.dt.uint8
+FP8X4 = mybir.dt.float8_e4m3fn_x4
+FP4X4 = mybir.dt.float4_e2m1fn_x4
+ALU = mybir.AluOpType
+ACT = mybir.ActivationFunctionType
+
+P = 128
+PACK = 4
+K_GROUP = P * PACK
+TOKENS = 128
+C = 16384
+GROUPS = C // K_GROUP
+HEADS = 24
+D = 64
+PAIRS = D // 2
+E = HEADS * D
+N_TILE = 512
+N_TILES = E // N_TILE
+TILE_HEADS = N_TILE // D
+TILE_BYTES = N_TILE * 2
+TILE_I32 = TILE_BYTES // 4
+
+EPS = 1e-6
+ROPE_BASE = 10000.0
+ROPE_AXES = ((D - 4 * (D // 6), 4, 7), (2 * (D // 6), 2, 3), (2 * (D // 6), 0, 3))
+
+X_LOAD_GROUPS = 8
+BANK_GROUPS = 2
+QUANT_GROUPS = 4
+WORDS_PER_GROUP = K_GROUP // 2
+
+CHUNK_GROUPS = 4
+TAPER_GROUPS = CHUNK_GROUPS * N_TILES
+W_BUFFERS = 6
+SCALE_RUN_GROUPS = 16
+SCALE_DMA_GROUPS = 8
+
+FLOPS = 2 * TOKENS * C * E
+
+
+def tile_attention_pa_k_kernel(tc, x, w_words, w_scales, b, norm_w, out):
+    nc = tc.nc
+    words_i32 = w_words.bitcast(I32)
+    scales_i32 = w_scales.bitcast(I32)
+
+    with ExitStack() as ctx:
+        ctx.enter_context(tc.manual_schedule())
+        const = ctx.enter_context(tc.tile_pool(name="const", bufs=1))
+        x_pool = ctx.enter_context(tc.tile_pool(name="x_pool", bufs=GROUPS // X_LOAD_GROUPS))
+        grouped_pool = ctx.enter_context(tc.tile_pool(name="grouped_pool", bufs=3))
+        w_pool = ctx.enter_context(tc.tile_pool(name="w_pool", bufs=W_BUFFERS))
+        tail = ctx.enter_context(tc.tile_pool(name="tail", bufs=2))
+        bank_pool = ctx.enter_context(tc.psum_pool(name="bank_pool", bufs=4))
+        acc_pool = ctx.enter_context(tc.psum_pool(name="acc_pool", bufs=1))
+
+        x_parts = []
+        for first in range(0, GROUPS, X_LOAD_GROUPS):
+            x_part = x_pool.tile([P, X_LOAD_GROUPS * K_GROUP], BF16)
+            nc.sync.dma_start(
+                out=x_part[:], in_=x[0, :, first * K_GROUP : (first + X_LOAD_GROUPS) * K_GROUP]
+            )
+            x_parts.append(x_part)
+
+        vector_rows = const.tile([P, E + D], BF16)
+        nc.vector.memset(vector_rows[:].bitcast(I32), 0)
+        nc.scalar.dma_start(out=vector_rows[0:1, 0:E], in_=b.unsqueeze(0))
+        nc.scalar.dma_start(out=vector_rows[0:1, E : E + D], in_=norm_w.unsqueeze(0))
+
+        identity = const.tile([P, P], F32)
+        make_identity(nc, identity[:])
+        ones = const.tile([P, P], BF16)
+        nc.gpsimd.memset(ones[:], 1.0)
+        token = const.tile([P, 1], I32)
+        nc.gpsimd.iota(token[:], pattern=[[0, 1]], base=0, channel_multiplier=1)
+
+        planes = const.tile([P, GROUPS, E], U8, align_bytes=64)
+        for first in range(0, GROUPS, SCALE_RUN_GROUPS):
+            nc.vector.memset(planes[:, first : first + SCALE_RUN_GROUPS, :].bitcast(I32), 0)
+
+        def load_scale_rows(first):
+            for g0 in range(first, first + SCALE_RUN_GROUPS, SCALE_DMA_GROUPS):
+                for a in range(2):
+                    for r in range(4):
+                        nc.sync.dma_start(
+                            out=planes[32 * a + r : P : 64, g0 : g0 + SCALE_DMA_GROUPS, :].bitcast(I32),
+                            in_=scales_i32[g0 : g0 + SCALE_DMA_GROUPS, 4 * a + r : 16 : 8, :].rearrange(
+                                "g q n -> q g n"
+                            ),
+                        )
+
+        pieces = []
+        for first in range(0, GROUPS - TAPER_GROUPS, CHUNK_GROUPS):
+            pieces.append((first, CHUNK_GROUPS, 0, N_TILES))
+        for c in range(N_TILES):
+            pieces.append((GROUPS - TAPER_GROUPS, TAPER_GROUPS, c, 1))
+
+        def load_piece(piece):
+            first, groups, c0, tiles = piece
+            if first % SCALE_RUN_GROUPS == 0:
+                load_scale_rows(first)
+            w_piece = w_pool.tile([P, groups, tiles * TILE_BYTES], U8, tag="w_piece", align_bytes=64)
+            nc.sync.dma_start(
+                out=w_piece[:].bitcast(I32),
+                in_=words_i32[
+                    first : first + groups, :, c0 * TILE_I32 : (c0 + tiles) * TILE_I32
+                ].rearrange("g p n -> p g n"),
+            )
+            return w_piece
+
+        w_pieces = []
+        for piece in pieces[: W_BUFFERS - 1]:
+            w_pieces.append(load_piece(piece))
+
+        x_codes = const.tile([P, GROUPS, TOKENS], U32, align_bytes=64)
+        x_scales = const.tile([P, GROUPS, TOKENS], U8, align_bytes=64)
+        for q0 in range(0, GROUPS, QUANT_GROUPS):
+            grouped = grouped_pool.tile([P, QUANT_GROUPS, TOKENS, PACK], BF16, align_bytes=64)
+            grouped_words = grouped[:].bitcast(F32)
+            for b0 in range(0, QUANT_GROUPS, BANK_GROUPS):
+                flipped = bank_pool.tile([P, BANK_GROUPS, 2, TOKENS], F32, tag="bank")
+                for i in range(BANK_GROUPS):
+                    g = q0 + b0 + i
+                    x_words = x_parts[g // X_LOAD_GROUPS][:].bitcast(F32)
+                    w0 = (g % X_LOAD_GROUPS) * WORDS_PER_GROUP
+                    for u in range(2):
+                        nc.tensor.transpose(
+                            out=flipped[:, i, u, :],
+                            in_=x_words[:, w0 + u : w0 + WORDS_PER_GROUP : 2],
+                            identity=identity[:],
+                        )
+                nc.scalar.copy(
+                    out=grouped_words[:, b0 : b0 + BANK_GROUPS, :, :],
+                    in_=flipped[:].rearrange("p g u n -> p g n u"),
+                )
+            nc.vector.quantize_mx(
+                out=x_codes[:, q0 : q0 + QUANT_GROUPS, :].rearrange("p g n -> p (g n)").bitcast(FP8X4),
+                scales=x_scales[:, q0 : q0 + QUANT_GROUPS, :].rearrange("p g n -> p (g n)"),
+                in_=grouped[:].rearrange("p g n t -> p (g n t)"),
+            )
+
+        bias_planes = const.tile([P, N_TILES, 2, N_TILE // 2], F32)
+        for c in range(N_TILES):
+            spread = bank_pool.tile([P, N_TILE], F32, tag="bank")
+            nc.tensor.matmul(
+                out=spread[:],
+                lhsT=ones[:],
+                rhs=vector_rows[:, c * N_TILE : (c + 1) * N_TILE],
+                start=True,
+                stop=True,
+            )
+            nc.scalar.copy(
+                out=bias_planes[:, c, :, :], in_=spread[:].rearrange("p (m two) -> p two m", two=2)
+            )
+        gain_planes = const.tile([P, 2, PAIRS], F32)
+        spread = bank_pool.tile([P, N_TILE], F32, tag="bank")
+        nc.tensor.matmul(
+            out=spread[:, 0:D], lhsT=ones[:], rhs=vector_rows[:, E : E + D], start=True, stop=True
+        )
+        nc.scalar.copy(
+            out=gain_planes[:], in_=spread[:, 0:D].rearrange("p (m two) -> p two m", two=2)
+        )
+
+        grid_i32 = const.tile([P, len(ROPE_AXES)], I32)
+        for axis, (channels, shift, mask) in enumerate(ROPE_AXES):
+            nc.vector.tensor_scalar(
+                out=grid_i32[:, axis : axis + 1],
+                in0=token[:],
+                scalar1=shift,
+                scalar2=mask,
+                op0=ALU.logical_shift_right,
+                op1=ALU.bitwise_and,
+            )
+        grid = const.tile([P, len(ROPE_AXES)], F32)
+        nc.vector.tensor_copy(out=grid[:], in_=grid_i32[:])
+
+        angles = const.tile([P, 2, PAIRS], F32)
+        pair = 0
+        for axis, (channels, shift, mask) in enumerate(ROPE_AXES):
+            for m in range(channels // 2):
+                nc.vector.tensor_scalar_mul(
+                    out=angles[:, 1, pair : pair + 1],
+                    in0=grid[:, axis : axis + 1],
+                    scalar1=1.0 / ROPE_BASE ** (2.0 * m / channels),
+                )
+                pair += 1
+        nc.vector.tensor_scalar_add(out=angles[:, 0, :], in0=angles[:, 1, :], scalar1=math.pi / 2.0)
+        turn = const.tile([P, 2, PAIRS], F32)
+        nc.vector.tensor_scalar(
+            out=turn[:],
+            in0=angles[:],
+            scalar1=math.pi,
+            scalar2=2.0 * math.pi,
+            op0=ALU.is_gt,
+            op1=ALU.mult,
+        )
+        nc.vector.tensor_sub(out=angles[:], in0=angles[:], in1=turn[:])
+        cos_sin = const.tile([P, 2, PAIRS], F32)
+        nc.scalar.activation(out=cos_sin[:], in_=angles[:], func=ACT.Sin)
+
+        keep = const.tile([P, 2, PAIRS], F32)
+        cross = const.tile([P, 2, PAIRS], F32)
+        for parity in range(2):
+            nc.vector.tensor_mul(out=keep[:, parity, :], in0=gain_planes[:, parity, :], in1=cos_sin[:, 0, :])
+            nc.vector.scalar_tensor_tensor(
+                out=cross[:, parity, :],
+                in0=gain_planes[:, parity, :],
+                scalar=1.0 - 2.0 * parity,
+                in1=cos_sin[:, 1, :],
+                op0=ALU.mult,
+                op1=ALU.mult,
+            )
+
+        eps = const.tile([P, 1], F32)
+        nc.vector.memset(eps[:], EPS)
+        table_warm = const.tile([P, 1], F32)
+        nc.scalar.sqrt(out=table_warm[:], in_=eps[:])
+
+        acc = [acc_pool.tile([P, N_TILE], F32, name="acc%d" % c) for c in range(N_TILES)]
+        plane_shape = [P, 2, TILE_HEADS, PAIRS]
+
+        def finish_column_tile(c):
+            y = tail.tile(plane_shape, F32)
+            nc.vector.tensor_tensor(
+                out=y[:].rearrange("p two h m -> p two (h m)"),
+                in0=acc[c][:].rearrange("p (hm two) -> p two hm", two=2),
+                in1=bias_planes[:, c, :, :],
+                op=ALU.add,
+            )
+            squares = tail.tile(plane_shape, F32)
+            nc.scalar.activation(out=squares[:], in_=y[:], func=ACT.Square)
+            kept = tail.tile(plane_shape, F32)
+            nc.vector.tensor_mul(
+                out=kept[:], in0=y[:], in1=keep[:].unsqueeze(2).to_broadcast(plane_shape)
+            )
+            crossed = tail.tile(plane_shape, F32)
+            nc.vector.tensor_mul(
+                out=crossed[:], in0=y[:], in1=cross[:].unsqueeze(2).to_broadcast(plane_shape)
+            )
+            sum_squares = tail.tile([P, TILE_HEADS], F32)
+            nc.vector.tensor_reduce(
+                out=sum_squares[:],
+                in_=squares[:].rearrange("p two h m -> p h two m"),
+                axis=mybir.AxisListType.XY,
+                op=ALU.add,
+            )
+            rms = tail.tile([P, TILE_HEADS], F32)
+            nc.scalar.activation(
+                out=rms[:], in_=sum_squares[:], func=ACT.Sqrt, bias=eps[:], scale=1.0 / D
+            )
+            turned = tail.tile(plane_shape, F32)
+            for parity in range(2):
+                nc.vector.tensor_add(
+                    out=turned[:, parity, :, :], in0=kept[:, parity, :, :], in1=crossed[:, 1 - parity, :, :]
+                )
+            inv_rms = tail.tile([P, TILE_HEADS], F32)
+            nc.vector.reciprocal(out=inv_rms[:], in_=rms[:])
+            result_shape = [P, TILE_HEADS, PAIRS, 2]
+            result = tail.tile(result_shape, F32)
+            nc.vector.tensor_mul(
+                out=result[:],
+                in0=turned[:].rearrange("p two h m -> p h m two"),
+                in1=inv_rms[:].unsqueeze(2).unsqueeze(3).to_broadcast(result_shape),
+            )
+            nc.sync.dma_start(
+                out=out[0, c * TILE_HEADS : (c + 1) * TILE_HEADS, :, :].rearrange("h n d -> n h d"),
+                in_=result[:].rearrange("p h m two -> p h (m two)"),
+            )
+
+        for index, piece in enumerate(pieces):
+            ahead = index + W_BUFFERS - 1
+            if ahead < len(pieces):
+                w_pieces.append(load_piece(pieces[ahead]))
+            first, groups, c0, tiles = piece
+            w_piece = w_pieces[index]
+            for i in range(groups):
+                g = first + i
+                for j in range(tiles):
+                    c = c0 + j
+                    nc.tensor.matmul_mx(
+                        out=acc[c][:],
+                        lhsT=x_codes[:, g, :].bitcast(FP8X4),
+                        lhsT_scale=x_scales[:, g, :],
+                        rhs=w_piece[:, i, j * TILE_BYTES : (j + 1) * TILE_BYTES].bitcast(FP4X4),
+                        rhs_scale=planes[:, g, c * N_TILE : (c + 1) * N_TILE],
+                        start=(g == 0),
+                        stop=(g == GROUPS - 1),
+                    )
+            if first + groups == GROUPS:
+                for j in range(tiles):
+                    finish_column_tile(c0 + j)

@@ -39,11 +39,12 @@ BANK_GROUPS = 2
 QUANT_GROUPS = 4
 WORDS_PER_GROUP = K_GROUP // 2
 
-CHUNK_GROUPS = 4
-TAPER_GROUPS = CHUNK_GROUPS * N_TILES
-W_BUFFERS = 6
+DMA_RUNS = 4
+CHUNK_GROUPS = DMA_RUNS
+TAPER_GROUPS = 12
 SCALE_RUN_GROUPS = 16
-SCALE_DMA_GROUPS = 8
+SCALE_DMA_GROUPS = DMA_RUNS
+W_BUFFERS = SCALE_RUN_GROUPS // CHUNK_GROUPS + 1
 
 FLOPS = 2 * TOKENS * C * E
 
@@ -84,7 +85,8 @@ def tile_attention_pa_k_kernel(tc, x, w_words, w_scales, b, norm_w, out):
         nc.gpsimd.iota(token[:], pattern=[[0, 1]], base=0, channel_multiplier=1)
 
         planes = const.tile([P, GROUPS, E], U8, align_bytes=64)
-        for first in range(0, GROUPS, SCALE_RUN_GROUPS):
+
+        def zero_planes(first):
             nc.vector.memset(planes[:, first : first + SCALE_RUN_GROUPS, :].bitcast(I32), 0)
 
         def load_scale_rows(first):
@@ -100,23 +102,25 @@ def tile_attention_pa_k_kernel(tc, x, w_words, w_scales, b, norm_w, out):
 
         pieces = []
         for first in range(0, GROUPS - TAPER_GROUPS, CHUNK_GROUPS):
-            pieces.append((first, CHUNK_GROUPS, 0, N_TILES))
+            pieces.append((first, 0, N_TILES))
         for c in range(N_TILES):
-            pieces.append((GROUPS - TAPER_GROUPS, TAPER_GROUPS, c, 1))
+            for first in range(GROUPS - TAPER_GROUPS, GROUPS, CHUNK_GROUPS):
+                pieces.append((first, c, 1))
 
         def load_piece(piece):
-            first, groups, c0, tiles = piece
+            first, c0, tiles = piece
             if first % SCALE_RUN_GROUPS == 0:
                 load_scale_rows(first)
-            w_piece = w_pool.tile([P, groups, tiles * TILE_BYTES], U8, tag="w_piece", align_bytes=64)
+            w_piece = w_pool.tile([P, CHUNK_GROUPS, tiles * TILE_BYTES], U8, tag="w_piece", align_bytes=64)
             nc.sync.dma_start(
                 out=w_piece[:].bitcast(I32),
                 in_=words_i32[
-                    first : first + groups, :, c0 * TILE_I32 : (c0 + tiles) * TILE_I32
+                    first : first + CHUNK_GROUPS, :, c0 * TILE_I32 : (c0 + tiles) * TILE_I32
                 ].rearrange("g p n -> p g n"),
             )
             return w_piece
 
+        zero_planes(0)
         w_pieces = []
         for piece in pieces[: W_BUFFERS - 1]:
             w_pieces.append(load_piece(piece))
@@ -147,6 +151,7 @@ def tile_attention_pa_k_kernel(tc, x, w_words, w_scales, b, norm_w, out):
                 scales=x_scales[:, q0 : q0 + QUANT_GROUPS, :].rearrange("p g n -> p (g n)"),
                 in_=grouped[:].rearrange("p g n t -> p (g n t)"),
             )
+        zero_planes(SCALE_RUN_GROUPS)
 
         bias_planes = const.tile([P, N_TILES, 2, N_TILE // 2], F32)
         for c in range(N_TILES):
@@ -271,18 +276,20 @@ def tile_attention_pa_k_kernel(tc, x, w_words, w_scales, b, norm_w, out):
                 in0=turned[:].rearrange("p two h m -> p h m two"),
                 in1=inv_rms[:].unsqueeze(2).unsqueeze(3).to_broadcast(result_shape),
             )
-            nc.sync.dma_start(
-                out=out[0, c * TILE_HEADS : (c + 1) * TILE_HEADS, :, :].rearrange("h n d -> n h d"),
-                in_=result[:].rearrange("p h m two -> p h (m two)"),
-            )
+            for h0 in range(0, TILE_HEADS, DMA_RUNS):
+                h_out = c * TILE_HEADS + h0
+                nc.sync.dma_start(
+                    out=out[0, h_out : h_out + DMA_RUNS, :, :].rearrange("h n d -> n h d"),
+                    in_=result[:, h0 : h0 + DMA_RUNS, :, :].rearrange("p h m two -> p h (m two)"),
+                )
 
         for index, piece in enumerate(pieces):
             ahead = index + W_BUFFERS - 1
             if ahead < len(pieces):
                 w_pieces.append(load_piece(pieces[ahead]))
-            first, groups, c0, tiles = piece
+            first, c0, tiles = piece
             w_piece = w_pieces[index]
-            for i in range(groups):
+            for i in range(CHUNK_GROUPS):
                 g = first + i
                 for j in range(tiles):
                     c = c0 + j
@@ -295,6 +302,6 @@ def tile_attention_pa_k_kernel(tc, x, w_words, w_scales, b, norm_w, out):
                         start=(g == 0),
                         stop=(g == GROUPS - 1),
                     )
-            if first + groups == GROUPS:
+            if first + CHUNK_GROUPS == GROUPS:
                 for j in range(tiles):
                     finish_column_tile(c0 + j)

@@ -39,11 +39,11 @@ BANK_GROUPS = 2
 QUANT_GROUPS = 4
 WORDS_PER_GROUP = K_GROUP // 2
 
-DMA_RUNS = 4
-CHUNK_GROUPS = DMA_RUNS
+CHUNK_GROUPS = 4
 TAPER_GROUPS = 12
 SCALE_RUN_GROUPS = 16
-SCALE_DMA_GROUPS = DMA_RUNS
+SCALE_DMA_GROUPS = 8
+STORE_HEADS = 4
 W_BUFFERS = SCALE_RUN_GROUPS // CHUNK_GROUPS + 1
 
 FLOPS = 2 * TOKENS * C * E
@@ -84,17 +84,21 @@ def tile_attention_pa_k_kernel(tc, x, w_words, w_scales, b, norm_w, out):
         token = const.tile([P, 1], I32)
         nc.gpsimd.iota(token[:], pattern=[[0, 1]], base=0, channel_multiplier=1)
 
-        planes = const.tile([P, GROUPS, E], U8, align_bytes=64)
+        planes = [
+            const.tile([P, SCALE_RUN_GROUPS, E], U8, name="planes%d" % run, align_bytes=64)
+            for run in range(GROUPS // SCALE_RUN_GROUPS)
+        ]
 
-        def zero_planes(first):
-            nc.vector.memset(planes[:, first : first + SCALE_RUN_GROUPS, :].bitcast(I32), 0)
+        def zero_planes(run):
+            nc.vector.memset(planes[run][:].bitcast(I32), 0)
 
-        def load_scale_rows(first):
-            for g0 in range(first, first + SCALE_RUN_GROUPS, SCALE_DMA_GROUPS):
+        def load_scale_rows(run):
+            for i0 in range(0, SCALE_RUN_GROUPS, SCALE_DMA_GROUPS):
+                g0 = run * SCALE_RUN_GROUPS + i0
                 for a in range(2):
                     for r in range(4):
                         nc.sync.dma_start(
-                            out=planes[32 * a + r : P : 64, g0 : g0 + SCALE_DMA_GROUPS, :].bitcast(I32),
+                            out=planes[run][32 * a + r : P : 64, i0 : i0 + SCALE_DMA_GROUPS, :].bitcast(I32),
                             in_=scales_i32[g0 : g0 + SCALE_DMA_GROUPS, 4 * a + r : 16 : 8, :].rearrange(
                                 "g q n -> q g n"
                             ),
@@ -110,7 +114,7 @@ def tile_attention_pa_k_kernel(tc, x, w_words, w_scales, b, norm_w, out):
         def load_piece(piece):
             first, c0, tiles = piece
             if first % SCALE_RUN_GROUPS == 0:
-                load_scale_rows(first)
+                load_scale_rows(first // SCALE_RUN_GROUPS)
             w_piece = w_pool.tile([P, CHUNK_GROUPS, tiles * TILE_BYTES], U8, tag="w_piece", align_bytes=64)
             nc.sync.dma_start(
                 out=w_piece[:].bitcast(I32),
@@ -151,7 +155,7 @@ def tile_attention_pa_k_kernel(tc, x, w_words, w_scales, b, norm_w, out):
                 scales=x_scales[:, q0 : q0 + QUANT_GROUPS, :].rearrange("p g n -> p (g n)"),
                 in_=grouped[:].rearrange("p g n t -> p (g n t)"),
             )
-        zero_planes(SCALE_RUN_GROUPS)
+        zero_planes(1)
 
         bias_planes = const.tile([P, N_TILES, 2, N_TILE // 2], F32)
         for c in range(N_TILES):
@@ -276,11 +280,11 @@ def tile_attention_pa_k_kernel(tc, x, w_words, w_scales, b, norm_w, out):
                 in0=turned[:].rearrange("p two h m -> p h m two"),
                 in1=inv_rms[:].unsqueeze(2).unsqueeze(3).to_broadcast(result_shape),
             )
-            for h0 in range(0, TILE_HEADS, DMA_RUNS):
+            for h0 in range(0, TILE_HEADS, STORE_HEADS):
                 h_out = c * TILE_HEADS + h0
                 nc.sync.dma_start(
-                    out=out[0, h_out : h_out + DMA_RUNS, :, :].rearrange("h n d -> n h d"),
-                    in_=result[:, h0 : h0 + DMA_RUNS, :, :].rearrange("p h m two -> p h (m two)"),
+                    out=out[0, h_out : h_out + STORE_HEADS, :, :].rearrange("h n d -> n h d"),
+                    in_=result[:, h0 : h0 + STORE_HEADS, :, :].rearrange("p h m two -> p h (m two)"),
                 )
 
         for index, piece in enumerate(pieces):
@@ -298,7 +302,9 @@ def tile_attention_pa_k_kernel(tc, x, w_words, w_scales, b, norm_w, out):
                         lhsT=x_codes[:, g, :].bitcast(FP8X4),
                         lhsT_scale=x_scales[:, g, :],
                         rhs=w_piece[:, i, j * TILE_BYTES : (j + 1) * TILE_BYTES].bitcast(FP4X4),
-                        rhs_scale=planes[:, g, c * N_TILE : (c + 1) * N_TILE],
+                        rhs_scale=planes[g // SCALE_RUN_GROUPS][
+                            :, g % SCALE_RUN_GROUPS, c * N_TILE : (c + 1) * N_TILE
+                        ],
                         start=(g == 0),
                         stop=(g == GROUPS - 1),
                     )

@@ -42,7 +42,7 @@ WORDS_PER_GROUP = K_GROUP // 2
 CHUNK_GROUPS = 4
 TAPER_GROUPS = 12
 SCALE_RUN_GROUPS = 16
-SCALE_DMA_GROUPS = 8
+SCALE_ROWS = K_GROUP // 32
 STORE_HEADS = 4
 W_BUFFERS = SCALE_RUN_GROUPS // CHUNK_GROUPS + 1
 
@@ -93,16 +93,14 @@ def tile_attention_pa_k_kernel(tc, x, w_words, w_scales, b, norm_w, out):
             nc.vector.memset(planes[run][:].bitcast(I32), 0)
 
         def load_scale_rows(run):
-            for i0 in range(0, SCALE_RUN_GROUPS, SCALE_DMA_GROUPS):
-                g0 = run * SCALE_RUN_GROUPS + i0
-                for a in range(2):
-                    for r in range(4):
-                        nc.sync.dma_start(
-                            out=planes[run][32 * a + r : P : 64, i0 : i0 + SCALE_DMA_GROUPS, :].bitcast(I32),
-                            in_=scales_i32[g0 : g0 + SCALE_DMA_GROUPS, 4 * a + r : 16 : 8, :].rearrange(
-                                "g q n -> q g n"
-                            ),
-                        )
+            g0 = run * SCALE_RUN_GROUPS
+            for low in range(SCALE_ROWS // 2):
+                for q in (low, low + SCALE_ROWS // 2):
+                    live = 32 * (q // 4) + q % 4
+                    nc.sync.dma_start(
+                        out=planes[run][live : live + 1, :, :].bitcast(I32),
+                        in_=scales_i32[g0 : g0 + SCALE_RUN_GROUPS, q : q + 1, :].rearrange("g q n -> q g n"),
+                    )
 
         pieces = []
         for first in range(0, GROUPS - TAPER_GROUPS, CHUNK_GROUPS):

@@ -52,7 +52,6 @@ FLOPS = 2 * TOKENS * C * E
 def tile_attention_pa_k_kernel(tc, x, w_words, w_scales, b, norm_w, out):
     nc = tc.nc
     words_i32 = w_words.bitcast(I32)
-    scales_i32 = w_scales.bitcast(I32)
 
     with ExitStack() as ctx:
         ctx.enter_context(tc.manual_schedule())
@@ -93,13 +92,16 @@ def tile_attention_pa_k_kernel(tc, x, w_words, w_scales, b, norm_w, out):
             nc.vector.memset(planes[run][:].bitcast(I32), 0)
 
         def load_scale_rows(run):
+            queue, raw = (nc.sync, I32) if run == 0 else (nc.gpsimd, F32)
             g0 = run * SCALE_RUN_GROUPS
             for low in range(SCALE_ROWS // 2):
                 for q in (low, low + SCALE_ROWS // 2):
                     live = 32 * (q // 4) + q % 4
-                    nc.sync.dma_start(
-                        out=planes[run][live : live + 1, :, :].bitcast(I32),
-                        in_=scales_i32[g0 : g0 + SCALE_RUN_GROUPS, q : q + 1, :].rearrange("g q n -> q g n"),
+                    queue.dma_start(
+                        out=planes[run][live : live + 1, :, :].bitcast(raw),
+                        in_=w_scales.bitcast(raw)[g0 : g0 + SCALE_RUN_GROUPS, q : q + 1, :].rearrange(
+                            "g q n -> q g n"
+                        ),
                     )
 
         pieces = []

@@ -44,7 +44,7 @@ TAPER_GROUPS = 12
 SCALE_RUN_GROUPS = 16
 SCALE_ROWS = K_GROUP // 32
 STORE_HEADS = 4
-W_BUFFERS = SCALE_RUN_GROUPS // CHUNK_GROUPS + 1
+W_BUFFERS = 6
 
 FLOPS = 2 * TOKENS * C * E
 
@@ -52,6 +52,7 @@ FLOPS = 2 * TOKENS * C * E
 def tile_attention_pa_k_kernel(tc, x, w_words, w_scales, b, norm_w, out):
     nc = tc.nc
     words_i32 = w_words.bitcast(I32)
+    scales_i32 = w_scales.bitcast(I32)
 
     with ExitStack() as ctx:
         ctx.enter_context(tc.manual_schedule())
@@ -88,20 +89,17 @@ def tile_attention_pa_k_kernel(tc, x, w_words, w_scales, b, norm_w, out):
             for run in range(GROUPS // SCALE_RUN_GROUPS)
         ]
 
-        def zero_planes(run):
+        for run in range(GROUPS // SCALE_RUN_GROUPS):
             nc.vector.memset(planes[run][:].bitcast(I32), 0)
 
         def load_scale_rows(run):
-            queue, raw = (nc.sync, I32) if run == 0 else (nc.gpsimd, F32)
             g0 = run * SCALE_RUN_GROUPS
             for low in range(SCALE_ROWS // 2):
                 for q in (low, low + SCALE_ROWS // 2):
                     live = 32 * (q // 4) + q % 4
-                    queue.dma_start(
-                        out=planes[run][live : live + 1, :, :].bitcast(raw),
-                        in_=w_scales.bitcast(raw)[g0 : g0 + SCALE_RUN_GROUPS, q : q + 1, :].rearrange(
-                            "g q n -> q g n"
-                        ),
+                    nc.sync.dma_start(
+                        out=planes[run][live : live + 1, :, :].bitcast(I32),
+                        in_=scales_i32[g0 : g0 + SCALE_RUN_GROUPS, q : q + 1, :].rearrange("g q n -> q g n"),
                     )
 
         pieces = []
@@ -124,7 +122,6 @@ def tile_attention_pa_k_kernel(tc, x, w_words, w_scales, b, norm_w, out):
             )
             return w_piece
 
-        zero_planes(0)
         w_pieces = []
         for piece in pieces[: W_BUFFERS - 1]:
             w_pieces.append(load_piece(piece))
@@ -155,7 +152,6 @@ def tile_attention_pa_k_kernel(tc, x, w_words, w_scales, b, norm_w, out):
                 scales=x_scales[:, q0 : q0 + QUANT_GROUPS, :].rearrange("p g n -> p (g n)"),
                 in_=grouped[:].rearrange("p g n t -> p (g n t)"),
             )
-        zero_planes(1)
 
         bias_planes = const.tile([P, N_TILES, 2, N_TILE // 2], F32)
         for c in range(N_TILES):
@@ -246,7 +242,14 @@ def tile_attention_pa_k_kernel(tc, x, w_words, w_scales, b, norm_w, out):
                 op=ALU.add,
             )
             squares = tail.tile(plane_shape, F32)
-            nc.scalar.activation(out=squares[:], in_=y[:], func=ACT.Square)
+            sum_squares = tail.tile([P, TILE_HEADS], F32)
+            for h in range(TILE_HEADS):
+                nc.scalar.activation(
+                    out=squares[:, :, h, :],
+                    in_=y[:, :, h, :],
+                    func=ACT.Square,
+                    accum_out=sum_squares[:, h : h + 1],
+                )
             kept = tail.tile(plane_shape, F32)
             nc.vector.tensor_mul(
                 out=kept[:], in0=y[:], in1=keep[:].unsqueeze(2).to_broadcast(plane_shape)
@@ -254,13 +257,6 @@ def tile_attention_pa_k_kernel(tc, x, w_words, w_scales, b, norm_w, out):
             crossed = tail.tile(plane_shape, F32)
             nc.vector.tensor_mul(
                 out=crossed[:], in0=y[:], in1=cross[:].unsqueeze(2).to_broadcast(plane_shape)
-            )
-            sum_squares = tail.tile([P, TILE_HEADS], F32)
-            nc.vector.tensor_reduce(
-                out=sum_squares[:],
-                in_=squares[:].rearrange("p two h m -> p h two m"),
-                axis=mybir.AxisListType.XY,
-                op=ALU.add,
             )
             rms = tail.tile([P, TILE_HEADS], F32)
             nc.scalar.activation(
@@ -280,6 +276,9 @@ def tile_attention_pa_k_kernel(tc, x, w_words, w_scales, b, norm_w, out):
                 in0=turned[:].rearrange("p two h m -> p h m two"),
                 in1=inv_rms[:].unsqueeze(2).unsqueeze(3).to_broadcast(result_shape),
             )
+            return result
+
+        def store_column_tile(c, result):
             for h0 in range(0, TILE_HEADS, STORE_HEADS):
                 h_out = c * TILE_HEADS + h0
                 nc.sync.dma_start(
@@ -287,6 +286,7 @@ def tile_attention_pa_k_kernel(tc, x, w_words, w_scales, b, norm_w, out):
                     in_=result[:, h0 : h0 + STORE_HEADS, :, :].rearrange("p h m two -> p h (m two)"),
                 )
 
+        unstored = []
         for index, piece in enumerate(pieces):
             ahead = index + W_BUFFERS - 1
             if ahead < len(pieces):
@@ -310,4 +310,8 @@ def tile_attention_pa_k_kernel(tc, x, w_words, w_scales, b, norm_w, out):
                     )
             if first + CHUNK_GROUPS == GROUPS:
                 for j in range(tiles):
-                    finish_column_tile(c0 + j)
+                    unstored.append((c0 + j, finish_column_tile(c0 + j)))
+            if ahead >= len(pieces) - 1:
+                for c, result in unstored:
+                    store_column_tile(c, result)
+                unstored = []

@@ -41,7 +41,6 @@ WORDS_PER_GROUP = K_GROUP // 2
 
 CHUNK_GROUPS = 4
 TAPER_GROUPS = 12
-SCALE_RUN_GROUPS = 16
 SCALE_ROWS = K_GROUP // 32
 STORE_HEADS = 4
 W_BUFFERS = 6
@@ -84,23 +83,15 @@ def tile_attention_pa_k_kernel(tc, x, w_words, w_scales, b, norm_w, out):
         token = const.tile([P, 1], I32)
         nc.gpsimd.iota(token[:], pattern=[[0, 1]], base=0, channel_multiplier=1)
 
-        planes = [
-            const.tile([P, SCALE_RUN_GROUPS, E], U8, name="planes%d" % run, align_bytes=64)
-            for run in range(GROUPS // SCALE_RUN_GROUPS)
-        ]
-
-        for run in range(GROUPS // SCALE_RUN_GROUPS):
-            nc.vector.memset(planes[run][:].bitcast(I32), 0)
-
-        def load_scale_rows(run):
-            g0 = run * SCALE_RUN_GROUPS
-            for low in range(SCALE_ROWS // 2):
-                for q in (low, low + SCALE_ROWS // 2):
-                    live = 32 * (q // 4) + q % 4
-                    nc.sync.dma_start(
-                        out=planes[run][live : live + 1, :, :].bitcast(I32),
-                        in_=scales_i32[g0 : g0 + SCALE_RUN_GROUPS, q : q + 1, :].rearrange("g q n -> q g n"),
-                    )
+        planes = const.tile([P, GROUPS, E], U8, align_bytes=64)
+        nc.vector.memset(planes[:].bitcast(I32), 0)
+        for low in range(SCALE_ROWS // 2):
+            for q in (low, low + SCALE_ROWS // 2):
+                live = 32 * (q // 4) + q % 4
+                nc.sync.dma_start(
+                    out=planes[live : live + 1, :, :].bitcast(I32),
+                    in_=scales_i32[:, q : q + 1, :].rearrange("g q n -> q g n"),
+                )
 
         pieces = []
         for first in range(0, GROUPS - TAPER_GROUPS, CHUNK_GROUPS):
@@ -111,8 +102,6 @@ def tile_attention_pa_k_kernel(tc, x, w_words, w_scales, b, norm_w, out):
 
         def load_piece(piece):
             first, c0, tiles = piece
-            if first % SCALE_RUN_GROUPS == 0:
-                load_scale_rows(first // SCALE_RUN_GROUPS)
             w_piece = w_pool.tile([P, CHUNK_GROUPS, tiles * TILE_BYTES], U8, tag="w_piece", align_bytes=64)
             nc.sync.dma_start(
                 out=w_piece[:].bitcast(I32),
@@ -302,9 +291,7 @@ def tile_attention_pa_k_kernel(tc, x, w_words, w_scales, b, norm_w, out):
                         lhsT=x_codes[:, g, :].bitcast(FP8X4),
                         lhsT_scale=x_scales[:, g, :],
                         rhs=w_piece[:, i, j * TILE_BYTES : (j + 1) * TILE_BYTES].bitcast(FP4X4),
-                        rhs_scale=planes[g // SCALE_RUN_GROUPS][
-                            :, g % SCALE_RUN_GROUPS, c * N_TILE : (c + 1) * N_TILE
-                        ],
+                        rhs_scale=planes[:, g, c * N_TILE : (c + 1) * N_TILE],
                         start=(g == 0),
                         stop=(g == GROUPS - 1),
                     )

@@ -258,21 +258,29 @@ def tile_attention_pa_k_kernel(tc, x, w_words, w_scales, b, norm_w, out):
                 )
             inv_rms = tail.tile([P, TILE_HEADS], F32)
             nc.vector.reciprocal(out=inv_rms[:], in_=rms[:])
-            result_shape = [P, TILE_HEADS, PAIRS, 2]
-            result = tail.tile(result_shape, F32)
+            half_shape = [P, STORE_HEADS, PAIRS, 2]
+            result_low = tail.tile(half_shape, F32)
             nc.vector.tensor_mul(
-                out=result[:],
-                in0=turned[:].rearrange("p two h m -> p h m two"),
-                in1=inv_rms[:].unsqueeze(2).unsqueeze(3).to_broadcast(result_shape),
+                out=result_low[:],
+                in0=turned[:, :, 0:STORE_HEADS, :].rearrange("p two h m -> p h m two"),
+                in1=inv_rms[:, 0:STORE_HEADS].unsqueeze(2).unsqueeze(3).to_broadcast(half_shape),
             )
-            return result
+            result_high = tail.tile(half_shape, F32)
+            for h in range(STORE_HEADS, TILE_HEADS):
+                nc.scalar.activation(
+                    out=result_high[:, h - STORE_HEADS, :, :],
+                    in_=turned[:, :, h, :].rearrange("p two m -> p m two"),
+                    func=ACT.Copy,
+                    scale=inv_rms[:, h : h + 1],
+                )
+            return (result_low, result_high)
 
         def store_column_tile(c, result):
-            for h0 in range(0, TILE_HEADS, STORE_HEADS):
-                h_out = c * TILE_HEADS + h0
+            for half in range(TILE_HEADS // STORE_HEADS):
+                h_out = c * TILE_HEADS + half * STORE_HEADS
                 nc.sync.dma_start(
                     out=out[0, h_out : h_out + STORE_HEADS, :, :].rearrange("h n d -> n h d"),
-                    in_=result[:, h0 : h0 + STORE_HEADS, :, :].rearrange("p h m two -> p h (m two)"),
+                    in_=result[half][:].rearrange("p h m two -> p h (m two)"),
                 )
 
         unstored = []

@@ -85,8 +85,8 @@ def tile_attention_pa_k_kernel(tc, x, w_words, w_scales, b, norm_w, out):
 
         planes = const.tile([P, GROUPS, E], U8, align_bytes=64)
         nc.vector.memset(planes[:].bitcast(I32), 0)
-        for low in range(SCALE_ROWS // 2):
-            for q in (low, low + SCALE_ROWS // 2):
+        for r in range(SCALE_ROWS // 4):
+            for q in (r, r + 8, r + 4, r + 12):
                 live = 32 * (q // 4) + q % 4
                 nc.sync.dma_start(
                     out=planes[live : live + 1, :, :].bitcast(I32),

@@ -95,18 +95,21 @@ def tile_attention_pa_k_kernel(tc, x, w_words, w_scales, b, norm_w, out):
 
         pieces = []
         for first in range(0, GROUPS - TAPER_GROUPS, CHUNK_GROUPS):
-            pieces.append((first, 0, N_TILES))
+            pieces.append((first, CHUNK_GROUPS, 0, N_TILES))
         for c in range(N_TILES):
             for first in range(GROUPS - TAPER_GROUPS, GROUPS, CHUNK_GROUPS):
-                pieces.append((first, c, 1))
+                pieces.append((first, CHUNK_GROUPS, c, 1))
+        first, groups, c, tiles = pieces[len(pieces) - 1]
+        pieces[len(pieces) - 1] = (first, groups // 2, c, tiles)
+        pieces.append((first + groups // 2, groups // 2, c, tiles))
 
         def load_piece(piece):
-            first, c0, tiles = piece
-            w_piece = w_pool.tile([P, CHUNK_GROUPS, tiles * TILE_BYTES], U8, tag="w_piece", align_bytes=64)
+            first, groups, c0, tiles = piece
+            w_piece = w_pool.tile([P, groups, tiles * TILE_BYTES], U8, tag="w_piece", align_bytes=64)
             nc.sync.dma_start(
                 out=w_piece[:].bitcast(I32),
                 in_=words_i32[
-                    first : first + CHUNK_GROUPS, :, c0 * TILE_I32 : (c0 + tiles) * TILE_I32
+                    first : first + groups, :, c0 * TILE_I32 : (c0 + tiles) * TILE_I32
                 ].rearrange("g p n -> p g n"),
             )
             return w_piece
@@ -288,9 +291,9 @@ def tile_attention_pa_k_kernel(tc, x, w_words, w_scales, b, norm_w, out):
             ahead = index + W_BUFFERS - 1
             if ahead < len(pieces):
                 w_pieces.append(load_piece(pieces[ahead]))
-            first, c0, tiles = piece
+            first, groups, c0, tiles = piece
             w_piece = w_pieces[index]
-            for i in range(CHUNK_GROUPS):
+            for i in range(groups):
                 g = first + i
                 for j in range(tiles):
                     c = c0 + j
@@ -303,7 +306,7 @@ def tile_attention_pa_k_kernel(tc, x, w_words, w_scales, b, norm_w, out):
                         start=(g == 0),
                         stop=(g == GROUPS - 1),
                     )
-            if first + CHUNK_GROUPS == GROUPS:
+            if first + groups == GROUPS:
                 for j in range(tiles):
                     unstored.append((c0 + j, finish_column_tile(c0 + j)))
             if ahead >= len(pieces) - 1:

@@ -66,7 +66,8 @@ def tile_attention_pa_k_kernel(tc, x, w_words, w_scales, b, norm_w, out):
         x_parts = []
         for first in range(0, GROUPS, X_LOAD_GROUPS):
             x_part = x_pool.tile([P, X_LOAD_GROUPS * K_GROUP], BF16)
-            nc.sync.dma_start(
+            queue = nc.sync if (first // X_LOAD_GROUPS) % 2 == 0 else nc.scalar
+            queue.dma_start(
                 out=x_part[:], in_=x[0, :, first * K_GROUP : (first + X_LOAD_GROUPS) * K_GROUP]
             )
             x_parts.append(x_part)

import math
from contextlib import ExitStack

import concourse.mybir as mybir
from concourse.masks import make_identity

F32 = mybir.dt.float32
BF16 = mybir.dt.bfloat16
I32 = mybir.dt.int32
U32 = mybir.dt.uint32
U8 = mybir.dt.uint8
FP8X4 = mybir.dt.float8_e4m3fn_x4
FP4X4 = mybir.dt.float4_e2m1fn_x4
ALU = mybir.AluOpType
ACT = mybir.ActivationFunctionType

P = 128
PACK = 4
K_GROUP = P * PACK
TOKENS = 128
C = 16384
GROUPS = C // K_GROUP
HEADS = 24
D = 64
PAIRS = D // 2
E = HEADS * D
N_TILE = 512
N_TILES = E // N_TILE
TILE_HEADS = N_TILE // D
TILE_BYTES = N_TILE * 2
TILE_I32 = TILE_BYTES // 4

EPS = 1e-6
ROPE_BASE = 10000.0
ROPE_AXES = ((D - 4 * (D // 6), 4, 7), (2 * (D // 6), 2, 3), (2 * (D // 6), 0, 3))

X_LOAD_GROUPS = 8
BANK_GROUPS = 2
QUANT_GROUPS = 4
WORDS_PER_GROUP = K_GROUP // 2

CHUNK_GROUPS = 4
TAPER_GROUPS = 12
SCALE_ROWS = K_GROUP // 32
STORE_HEADS = 4
W_BUFFERS = 6

FLOPS = 2 * TOKENS * C * E


def tile_attention_pa_k_kernel(tc, x, w_words, w_scales, b, norm_w, out):
    nc = tc.nc
    words_i32 = w_words.bitcast(I32)
    scales_i32 = w_scales.bitcast(I32)

    with ExitStack() as ctx:
        ctx.enter_context(tc.manual_schedule())
        const = ctx.enter_context(tc.tile_pool(name="const", bufs=1))
        x_pool = ctx.enter_context(tc.tile_pool(name="x_pool", bufs=GROUPS // X_LOAD_GROUPS))
        grouped_pool = ctx.enter_context(tc.tile_pool(name="grouped_pool", bufs=3))
        w_pool = ctx.enter_context(tc.tile_pool(name="w_pool", bufs=W_BUFFERS))
        tail = ctx.enter_context(tc.tile_pool(name="tail", bufs=2))
        bank_pool = ctx.enter_context(tc.psum_pool(name="bank_pool", bufs=4))
        acc_pool = ctx.enter_context(tc.psum_pool(name="acc_pool", bufs=1))

        x_parts = []
        for first in range(0, GROUPS, X_LOAD_GROUPS):
            x_part = x_pool.tile([P, X_LOAD_GROUPS * K_GROUP], BF16)
            queue = nc.sync if (first // X_LOAD_GROUPS) % 2 == 0 else nc.scalar
            queue.dma_start(
                out=x_part[:], in_=x[0, :, first * K_GROUP : (first + X_LOAD_GROUPS) * K_GROUP]
            )
            x_parts.append(x_part)

        vector_rows = const.tile([P, E + D], BF16)
        nc.vector.memset(vector_rows[:].bitcast(I32), 0)
        nc.scalar.dma_start(out=vector_rows[0:1, 0:E], in_=b.unsqueeze(0))
        nc.scalar.dma_start(out=vector_rows[0:1, E : E + D], in_=norm_w.unsqueeze(0))

        identity = const.tile([P, P], F32)
        make_identity(nc, identity[:])
        ones = const.tile([P, P], BF16)
        nc.gpsimd.memset(ones[:], 1.0)
        token = const.tile([P, 1], I32)
        nc.gpsimd.iota(token[:], pattern=[[0, 1]], base=0, channel_multiplier=1)

        planes = const.tile([P, GROUPS, E], U8, align_bytes=64)
        nc.vector.memset(planes[:].bitcast(I32), 0)
        for r in range(SCALE_ROWS // 4):
            for q in (r, r + 8, r + 4, r + 12):
                live = 32 * (q // 4) + q % 4
                nc.sync.dma_start(
                    out=planes[live : live + 1, :, :].bitcast(I32),
                    in_=scales_i32[:, q : q + 1, :].rearrange("g q n -> q g n"),
                )

        pieces = []
        for first in range(0, GROUPS - TAPER_GROUPS, CHUNK_GROUPS):
            pieces.append((first, CHUNK_GROUPS, 0, N_TILES))
        for c in range(N_TILES):
            for first in range(GROUPS - TAPER_GROUPS, GROUPS, CHUNK_GROUPS):
                pieces.append((first, CHUNK_GROUPS, c, 1))
        first, groups, c, tiles = pieces[len(pieces) - 1]
        pieces[len(pieces) - 1] = (first, groups // 2, c, tiles)
        pieces.append((first + groups // 2, groups // 2, c, tiles))

        def load_piece(piece):
            first, groups, c0, tiles = piece
            w_piece = w_pool.tile([P, groups, tiles * TILE_BYTES], U8, tag="w_piece", align_bytes=64)
            nc.sync.dma_start(
                out=w_piece[:].bitcast(I32),
                in_=words_i32[
                    first : first + groups, :, c0 * TILE_I32 : (c0 + tiles) * TILE_I32
                ].rearrange("g p n -> p g n"),
            )
            return w_piece

        w_pieces = []
        for piece in pieces[: W_BUFFERS - 1]:
            w_pieces.append(load_piece(piece))

        x_codes = const.tile([P, GROUPS, TOKENS], U32, align_bytes=64)
        x_scales = const.tile([P, GROUPS, TOKENS], U8, align_bytes=64)
        for q0 in range(0, GROUPS, QUANT_GROUPS):
            grouped = grouped_pool.tile([P, QUANT_GROUPS, TOKENS, PACK], BF16, align_bytes=64)
            grouped_words = grouped[:].bitcast(F32)
            for b0 in range(0, QUANT_GROUPS, BANK_GROUPS):
                flipped = bank_pool.tile([P, BANK_GROUPS, 2, TOKENS], F32, tag="bank")
                for i in range(BANK_GROUPS):
                    g = q0 + b0 + i
                    x_words = x_parts[g // X_LOAD_GROUPS][:].bitcast(F32)
                    w0 = (g % X_LOAD_GROUPS) * WORDS_PER_GROUP
                    for u in range(2):
                        nc.tensor.transpose(
                            out=flipped[:, i, u, :],
                            in_=x_words[:, w0 + u : w0 + WORDS_PER_GROUP : 2],
                            identity=identity[:],
                        )
                nc.scalar.copy(
                    out=grouped_words[:, b0 : b0 + BANK_GROUPS, :, :],
                    in_=flipped[:].rearrange("p g u n -> p g n u"),
                )
            nc.vector.quantize_mx(
                out=x_codes[:, q0 : q0 + QUANT_GROUPS, :].rearrange("p g n -> p (g n)").bitcast(FP8X4),
                scales=x_scales[:, q0 : q0 + QUANT_GROUPS, :].rearrange("p g n -> p (g n)"),
                in_=grouped[:].rearrange("p g n t -> p (g n t)"),
            )

        bias_planes = const.tile([P, N_TILES, 2, N_TILE // 2], F32)
        for c in range(N_TILES):
            spread = bank_pool.tile([P, N_TILE], F32, tag="bank")
            nc.tensor.matmul(
                out=spread[:],
                lhsT=ones[:],
                rhs=vector_rows[:, c * N_TILE : (c + 1) * N_TILE],
                start=True,
                stop=True,
            )
            nc.scalar.copy(
                out=bias_planes[:, c, :, :], in_=spread[:].rearrange("p (m two) -> p two m", two=2)
            )
        gain_planes = const.tile([P, 2, PAIRS], F32)
        spread = bank_pool.tile([P, N_TILE], F32, tag="bank")
        nc.tensor.matmul(
            out=spread[:, 0:D], lhsT=ones[:], rhs=vector_rows[:, E : E + D], start=True, stop=True
        )
        nc.scalar.copy(
            out=gain_planes[:], in_=spread[:, 0:D].rearrange("p (m two) -> p two m", two=2)
        )

        grid_i32 = const.tile([P, len(ROPE_AXES)], I32)
        for axis, (channels, shift, mask) in enumerate(ROPE_AXES):
            nc.vector.tensor_scalar(
                out=grid_i32[:, axis : axis + 1],
                in0=token[:],
                scalar1=shift,
                scalar2=mask,
                op0=ALU.logical_shift_right,
                op1=ALU.bitwise_and,
            )
        grid = const.tile([P, len(ROPE_AXES)], F32)
        nc.vector.tensor_copy(out=grid[:], in_=grid_i32[:])

        angles = const.tile([P, 2, PAIRS], F32)
        pair = 0
        for axis, (channels, shift, mask) in enumerate(ROPE_AXES):
            for m in range(channels // 2):
                nc.vector.tensor_scalar_mul(
                    out=angles[:, 1, pair : pair + 1],
                    in0=grid[:, axis : axis + 1],
                    scalar1=1.0 / ROPE_BASE ** (2.0 * m / channels),
                )
                pair += 1
        nc.vector.tensor_scalar_add(out=angles[:, 0, :], in0=angles[:, 1, :], scalar1=math.pi / 2.0)
        turn = const.tile([P, 2, PAIRS], F32)
        nc.vector.tensor_scalar(
            out=turn[:],
            in0=angles[:],
            scalar1=math.pi,
            scalar2=2.0 * math.pi,
            op0=ALU.is_gt,
            op1=ALU.mult,
        )
        nc.vector.tensor_sub(out=angles[:], in0=angles[:], in1=turn[:])
        cos_sin = const.tile([P, 2, PAIRS], F32)
        nc.scalar.activation(out=cos_sin[:], in_=angles[:], func=ACT.Sin)

        keep = const.tile([P, 2, PAIRS], F32)
        cross = const.tile([P, 2, PAIRS], F32)
        for parity in range(2):
            nc.vector.tensor_mul(out=keep[:, parity, :], in0=gain_planes[:, parity, :], in1=cos_sin[:, 0, :])
            nc.vector.scalar_tensor_tensor(
                out=cross[:, parity, :],
                in0=gain_planes[:, parity, :],
                scalar=1.0 - 2.0 * parity,
                in1=cos_sin[:, 1, :],
                op0=ALU.mult,
                op1=ALU.mult,
            )

        eps = const.tile([P, 1], F32)
        nc.vector.memset(eps[:], EPS)
        table_warm = const.tile([P, 1], F32)
        nc.scalar.sqrt(out=table_warm[:], in_=eps[:])

        acc = [acc_pool.tile([P, N_TILE], F32, name="acc%d" % c) for c in range(N_TILES)]
        plane_shape = [P, 2, TILE_HEADS, PAIRS]

        def finish_column_tile(c):
            y = tail.tile(plane_shape, F32)
            nc.vector.tensor_tensor(
                out=y[:].rearrange("p two h m -> p two (h m)"),
                in0=acc[c][:].rearrange("p (hm two) -> p two hm", two=2),
                in1=bias_planes[:, c, :, :],
                op=ALU.add,
            )
            squares = tail.tile(plane_shape, F32)
            sum_squares = tail.tile([P, TILE_HEADS], F32)
            for h in range(TILE_HEADS):
                nc.scalar.activation(
                    out=squares[:, :, h, :],
                    in_=y[:, :, h, :],
                    func=ACT.Square,
                    accum_out=sum_squares[:, h : h + 1],
                )
            kept = tail.tile(plane_shape, F32)
            nc.vector.tensor_mul(
                out=kept[:], in0=y[:], in1=keep[:].unsqueeze(2).to_broadcast(plane_shape)
            )
            crossed = tail.tile(plane_shape, F32)
            nc.vector.tensor_mul(
                out=crossed[:], in0=y[:], in1=cross[:].unsqueeze(2).to_broadcast(plane_shape)
            )
            rms = tail.tile([P, TILE_HEADS], F32)
            nc.scalar.activation(
                out=rms[:], in_=sum_squares[:], func=ACT.Sqrt, bias=eps[:], scale=1.0 / D
            )
            turned = tail.tile(plane_shape, F32)
            for parity in range(2):
                nc.vector.tensor_add(
                    out=turned[:, parity, :, :], in0=kept[:, parity, :, :], in1=crossed[:, 1 - parity, :, :]
                )
            inv_rms = tail.tile([P, TILE_HEADS], F32)
            nc.vector.reciprocal(out=inv_rms[:], in_=rms[:])
            half_shape = [P, STORE_HEADS, PAIRS, 2]
            result_low = tail.tile(half_shape, F32)
            nc.vector.tensor_mul(
                out=result_low[:],
                in0=turned[:, :, 0:STORE_HEADS, :].rearrange("p two h m -> p h m two"),
                in1=inv_rms[:, 0:STORE_HEADS].unsqueeze(2).unsqueeze(3).to_broadcast(half_shape),
            )
            result_high = tail.tile(half_shape, F32)
            for h in range(STORE_HEADS, TILE_HEADS):
                nc.scalar.activation(
                    out=result_high[:, h - STORE_HEADS, :, :],
                    in_=turned[:, :, h, :].rearrange("p two m -> p m two"),
                    func=ACT.Copy,
                    scale=inv_rms[:, h : h + 1],
                )
            return (result_low, result_high)

        def store_column_tile(c, result):
            for half in range(TILE_HEADS // STORE_HEADS):
                h_out = c * TILE_HEADS + half * STORE_HEADS
                nc.sync.dma_start(
                    out=out[0, h_out : h_out + STORE_HEADS, :, :].rearrange("h n d -> n h d"),
                    in_=result[half][:].rearrange("p h m two -> p h (m two)"),
                )

        unstored = []
        for index, piece in enumerate(pieces):
            ahead = index + W_BUFFERS - 1
            if ahead < len(pieces):
                w_pieces.append(load_piece(pieces[ahead]))
            first, groups, c0, tiles = piece
            w_piece = w_pieces[index]
            for i in range(groups):
                g = first + i
                for j in range(tiles):
                    c = c0 + j
                    nc.tensor.matmul_mx(
                        out=acc[c][:],
                        lhsT=x_codes[:, g, :].bitcast(FP8X4),
                        lhsT_scale=x_scales[:, g, :],
                        rhs=w_piece[:, i, j * TILE_BYTES : (j + 1) * TILE_BYTES].bitcast(FP4X4),
                        rhs_scale=planes[:, g, c * N_TILE : (c + 1) * N_TILE],
                        start=(g == 0),
                        stop=(g == GROUPS - 1),
                    )
            if first + groups == GROUPS:
                for j in range(tiles):
                    unstored.append((c0 + j, finish_column_tile(c0 + j)))
            if ahead >= len(pieces) - 1:
                for c, result in unstored:
                    store_column_tile(c, result)
                unstored = []
